import numpy as np
import ml_dtypes


def mxq(x, axis, fmt="e4m3"):
    dtype, down = {"e4m3": (ml_dtypes.float8_e4m3fn, 7), "e5m2": (ml_dtypes.float8_e5m2, 14)}[fmt]
    v = np.moveaxis(np.asarray(x, np.float32).astype(ml_dtypes.bfloat16).astype(np.float64), axis, -1)
    blocks = v.reshape(v.shape[:-1] + (-1, 32))
    amax = np.abs(blocks).max(-1, keepdims=True)
    byte = np.maximum(np.where(amax > 0, np.frexp(amax)[1] - 1 + 127, 0) - down, 1)
    scale = np.exp2(byte - 127.0)
    codes = (blocks / scale).astype(np.float32).astype(dtype).astype(np.float64)
    return np.moveaxis((codes * scale).reshape(v.shape), -1, axis)


WIDE = False


def mx_kscale(k):
    if not WIDE:
        return np.ones(k)
    levels = np.array([10, -10, 5, -5, 0])
    a = np.random.permutation(np.resize(levels, k // 512 * 4)).reshape(k // 512, 4)
    idx = np.arange(k)
    return np.exp2(a[idx // 512, idx % 128 // 32])


BF16 = ml_dtypes.bfloat16


def bf(x):
    return np.asarray(x, np.float32).astype(BF16)


def f64(x):
    return np.asarray(x).astype(np.float64)


B, N, HD, NH, KVH, D = 1, 512, 2048, 16, 4, 128
QD = NH * D
KVD = KVH * D
EPS = 2.0 ** -23


def setup_inputs():
    s = mx_kscale(HD)
    rows = np.exp2(np.random.uniform(-2.0, 2.0, (B, N, 1)))
    rows = np.where(np.random.random((B, N, 1)) < 0.125, rows * 2.0 ** -11, rows)
    return {"tokens": bf(np.random.standard_normal((B, N, HD)) * rows),
            "norm_w": bf((1.0 + 0.1 * np.random.standard_normal(HD)) * s),
            "Wq": bf(np.random.standard_normal((QD, HD)) * 0.4 / np.sqrt(HD) / s[None, :]),
            "bq": bf(np.random.standard_normal(QD) * 0.1),
            "Wk": bf(np.random.standard_normal((KVD, HD)) * 0.4 / np.sqrt(HD) / s[None, :]),
            "bk": bf(np.random.standard_normal(KVD) * 0.1),
            "Wv": bf(np.random.standard_normal((KVD, HD)) / np.sqrt(HD) / s[None, :]),
            "bv": bf(np.random.standard_normal(KVD) * 0.3)}


def reference(tokens, norm_w, Wq, bq, Wk, bk, Wv, bv):
    t = f64(tokens)
    x = t / np.sqrt(np.mean(t * t, axis=-1, keepdims=True) + EPS) * f64(norm_w)
    xq = mxq(x, 2, "e4m3")
    q = ((xq @ mxq(f64(Wq), 1, "e4m3").T) + f64(bq)).reshape(B, N, NH, D).transpose(0, 2, 1, 3)
    k = ((xq @ mxq(f64(Wk), 1, "e4m3").T) + f64(bk)).reshape(B, N, KVH, D).transpose(0, 2, 1, 3)
    v = ((xq @ mxq(f64(Wv), 1, "e4m3").T) + f64(bv)).reshape(B, N, KVH, D).transpose(0, 2, 1, 3)
    return q, k, v

@@ -1,0 +1,253 @@
+from contextlib import ExitStack
+
+import concourse.mybir as mybir
+from concourse.masks import make_identity
+
+F32 = mybir.dt.float32
+BF16 = mybir.dt.bfloat16
+I32 = mybir.dt.int32
+U32 = mybir.dt.uint32
+U8 = mybir.dt.uint8
+FP8X4 = mybir.dt.float8_e4m3fn_x4
+ACT = mybir.ActivationFunctionType
+ALU = mybir.AluOpType
+
+P = 128
+PACK = 4
+K_PASS = P * PACK
+N_TOK = 512
+HD = 2048
+PASSES = HD // K_PASS
+TOK_TILES = N_TOK // P
+GROUP = 512
+HEADS = GROUP // P
+Q_GROUPS = 4
+GROUPS = Q_GROUPS + 2
+RAW_GROUPS = 3
+EPS = 2.0 ** -23
+
+FLOPS = 2 * N_TOK * GROUPS * GROUP * HD
+
+
+def tile_attentionlayerdecoder_pa_kernel(
+    tc, tokens, norm_w, Wq, bq, Wk, bk, Wv, bv, out_0, out_1, out_2
+):
+    nc = tc.nc
+    token_rows = tokens.rearrange("b n k -> (b n) k")
+    q_heads = out_0.rearrange("b h n d -> (b h) n d")
+
+    group_rows = [Wq[q * GROUP : (q + 1) * GROUP, :] for q in range(Q_GROUPS)] + [Wk, Wv]
+    group_heads = [q_heads[q * HEADS : (q + 1) * HEADS, :, :] for q in range(Q_GROUPS)] + [
+        out_1.rearrange("b h n d -> (b h) n d"),
+        out_2.rearrange("b h n d -> (b h) n d"),
+    ]
+
+    with ExitStack() as ctx:
+        keep = ctx.enter_context(tc.tile_pool(name="keep", bufs=1))
+        raw_pool = ctx.enter_context(tc.tile_pool(name="raw", bufs=RAW_GROUPS * HEADS))
+        stats = ctx.enter_context(tc.tile_pool(name="stats", bufs=TOK_TILES))
+        rows_pool = ctx.enter_context(tc.tile_pool(name="rows", bufs=2))
+        grouped_pool = ctx.enter_context(tc.tile_pool(name="grouped", bufs=PASSES))
+        result_pool = ctx.enter_context(tc.tile_pool(name="result", bufs=8))
+        psum = ctx.enter_context(tc.psum_pool(name="psum", bufs=8))
+        ctx.enter_context(tc.manual_schedule())
+
+        gain_row = keep.tile([P, HD], BF16)
+        nc.vector.memset(gain_row[:].bitcast(I32), 0)
+        ones = keep.tile([P, P], BF16)
+        nc.vector.memset(ones[:], 1.0)
+        eps_col = keep.tile([P, 1], F32)
+        nc.vector.memset(eps_col[:], EPS)
+        bias_row = keep.tile([P, GROUPS * GROUP], BF16)
+        nc.vector.memset(bias_row[:].bitcast(I32), 0)
+        ident_bf16 = keep.tile([P, P], BF16)
+        make_identity(nc, ident_bf16[:])
+        ident_f32 = keep.tile([P, P], F32)
+        make_identity(nc, ident_f32[:])
+
+        warm = keep.tile([P, 1], F32)
+        nc.scalar.activation(out=warm[:], in_=eps_col[:], func=ACT.Sqrt)
+
+        def load_gain():
+            nc.sync.dma_start(out=gain_row[0:1, :], in_=norm_w.rearrange("(o k) -> o k", o=1))
+
+        def load_biases():
+            first = 0
+            for bias in (bq, bk, bv):
+                width = bias.shape[0]
+                nc.sync.dma_start(
+                    out=bias_row[0:1, first : first + width],
+                    in_=bias.rearrange("(o c) -> o c", o=1),
+                )
+                first += width
+
+        gain_all = keep.tile([P, HD], BF16)
+        bias_all = keep.tile([P, GROUPS * GROUP], F32)
+        x_codes = keep.tile([P, TOK_TILES, PASSES, P], U32, align_bytes=64)
+        x_scales = keep.tile([P, TOK_TILES, PASSES, P], U8, align_bytes=64)
+        w_codes = [
+            keep.tile([P, PASSES, GROUP], U32, name="w_codes%d" % j, align_bytes=64)
+            for j in range(GROUPS)
+        ]
+        w_scales = [
+            keep.tile([P, PASSES, GROUP], U8, name="w_scales%d" % j, align_bytes=64)
+            for j in range(GROUPS)
+        ]
+        token_tiles = [keep.tile([P, HD], BF16, name="tokens%d" % i) for i in range(TOK_TILES)]
+        raw_heads = {}
+
+        def load_tokens(i):
+            nc.sync.dma_start(out=token_tiles[i][:], in_=token_rows[i * P : (i + 1) * P, :])
+
+        def load_weights(j):
+            for h in range(HEADS):
+                head = raw_pool.tile([P, HD], BF16, name="raw_head", tag="raw_head")
+                nc.sync.dma_start(out=head[:], in_=group_rows[j][h * P : (h + 1) * P, :])
+                raw_heads[(j, h)] = head
+
+        def broadcast_gain():
+            for c in range(HD // GROUP):
+                cols = slice(c * GROUP, (c + 1) * GROUP)
+                bank = psum.tile([P, GROUP], F32, tag="bank")
+                nc.tensor.matmul(out=bank[:], lhsT=ones[:], rhs=gain_row[:, cols], start=True, stop=True)
+                nc.vector.tensor_copy(out=gain_all[:, cols], in_=bank[:])
+
+        def broadcast_bias(j):
+            cols = slice(j * GROUP, (j + 1) * GROUP)
+            bank = psum.tile([P, GROUP], F32, tag="bank")
+            nc.tensor.matmul(out=bank[:], lhsT=ones[:], rhs=bias_row[:, cols], start=True, stop=True)
+            nc.scalar.copy(out=bias_all[:, cols], in_=bank[:])
+
+        def normalise(i):
+            squares = rows_pool.tile([P, HD], BF16, tag="squares")
+            sum_sq = stats.tile([P, 1], F32, tag="sum_sq")
+            nc.scalar.activation(
+                out=squares[:], in_=token_tiles[i][:], func=ACT.Square, accum_out=sum_sq[:]
+            )
+            rms = stats.tile([P, 1], F32, tag="rms")
+            nc.scalar.activation(
+                out=rms[:], in_=sum_sq[:], func=ACT.Sqrt, scale=1.0 / HD, bias=eps_col[:]
+            )
+            rstd = stats.tile([P, 1], F32, tag="rstd")
+            nc.vector.reciprocal(out=rstd[:], in_=rms[:])
+            x_rows = rows_pool.tile([P, HD], BF16, tag="x_rows")
+            by_parity = "n (c p e) -> n c p e"
+            for e in range(2):
+                nc.vector.scalar_tensor_tensor(
+                    out=x_rows[:].rearrange("n (c e p) -> n c e p", e=2, p=P)[:, :, e, :],
+                    in0=token_tiles[i][:].rearrange(by_parity, p=P, e=2)[:, :, :, e],
+                    scalar=rstd[:, 0:1],
+                    in1=gain_all[:].rearrange(by_parity, p=P, e=2)[:, :, :, e],
+                    op0=ALU.mult,
+                    op1=ALU.mult,
+                )
+            return x_rows
+
+        def pack_tokens(i, x_rows):
+            grouped = rows_pool.tile([P, PASSES, P, PACK], BF16, tag="grouped_x", align_bytes=64)
+            for g in range(PASSES):
+                bank = psum.tile([P, PACK, P], BF16, tag="bank")
+                for t in range(PACK):
+                    first = (g * PACK + t) * P
+                    nc.tensor.transpose(
+                        out=bank[:, t, :], in_=x_rows[:, first : first + P], identity=ident_bf16[:]
+                    )
+                copy = nc.scalar.copy if g % 2 == 0 else nc.vector.tensor_copy
+                copy(out=grouped[:, g, :, :], in_=bank[:].rearrange("p t n -> p n t"))
+            nc.vector.quantize_mx(
+                out=x_codes[:, i, :, :].rearrange("p g n -> p (g n)").bitcast(FP8X4),
+                scales=x_scales[:, i, :, :].rearrange("p g n -> p (g n)"),
+                in_=grouped[:].rearrange("p g n t -> p (g n t)"),
+            )
+
+        def transpose_weights(j, g):
+            grouped = grouped_pool.tile([P, GROUP * PACK], BF16, tag="grouped_w", align_bytes=64)
+            words = grouped[:].bitcast(F32).rearrange("p (o u) -> p o u", u=2)
+            for pair in range(HEADS // 2):
+                bank = psum.tile([P, 2, 2 * P], F32, tag="bank")
+                for u in range(2):
+                    first = (2 * g + u) * P
+                    for r in range(2):
+                        nc.tensor.transpose(
+                            out=bank[:, u, r * P : (r + 1) * P],
+                            in_=raw_heads[(j, 2 * pair + r)][:].bitcast(F32)[:, first : first + P],
+                            identity=ident_f32[:],
+                        )
+                nc.scalar.copy(
+                    out=words[:, 2 * pair * P : 2 * (pair + 1) * P, :],
+                    in_=bank[:].rearrange("p u o -> p o u"),
+                )
+            return grouped
+
+        def quantise_weights(j, g, grouped):
+            nc.vector.quantize_mx(
+                out=w_codes[j][:, g, :].bitcast(FP8X4), scales=w_scales[j][:, g, :], in_=grouped[:]
+            )
+
+        def multiply(i, j, store_queue):
+            bank = psum.tile([P, GROUP], F32, tag="bank")
+            for g in range(PASSES):
+                nc.tensor.matmul_mx(
+                    out=bank[:],
+                    lhsT=x_codes[:, i, g, :].bitcast(FP8X4),
+                    lhsT_scale=x_scales[:, i, g, :],
+                    rhs=w_codes[j][:, g, :].bitcast(FP8X4),
+                    rhs_scale=w_scales[j][:, g, :],
+                    start=(g == 0),
+                    stop=(g == PASSES - 1),
+                )
+            result = result_pool.tile([P, GROUP], F32, tag="result")
+            nc.vector.tensor_tensor(
+                out=result[:], in0=bank[:], in1=bias_all[:, j * GROUP : (j + 1) * GROUP], op=ALU.add
+            )
+            store_queue.dma_start(
+                out=group_heads[j][:, i * P : (i + 1) * P, :].rearrange("h n d -> n h d"),
+                in_=result[:].rearrange("n (h d) -> n h d", h=HEADS),
+            )
+
+        def prepare_weights(j, half):
+            passes = (2 * half, 2 * half + 1)
+            grouped = [transpose_weights(j, g) for g in passes]
+            for g, tile_g in zip(passes, grouped):
+                quantise_weights(j, g, tile_g)
+
+        load_gain()
+        load_tokens(0)
+        load_tokens(1)
+        load_biases()
+        load_weights(0)
+        load_tokens(2)
+        load_tokens(3)
+        for j in range(1, RAW_GROUPS):
+            load_weights(j)
+
+        broadcast_gain()
+        x_rows_0 = normalise(0)
+        x_rows_1 = normalise(1)
+        pack_tokens(0, x_rows_0)
+        broadcast_bias(0)
+        prepare_weights(0, 0)
+        pack_tokens(1, x_rows_1)
+        prepare_weights(0, 1)
+        load_weights(RAW_GROUPS)
+
+        late_rows = None
+        for j in range(GROUPS):
+            if j + 1 < GROUPS:
+                broadcast_bias(j + 1)
+            for half in range(2):
+                if j + 1 < GROUPS:
+                    prepare_weights(j + 1, half)
+                multiply(half, j, nc.gpsimd)
+            if j + 1 + RAW_GROUPS < GROUPS:
+                load_weights(j + 1 + RAW_GROUPS)
+            late = 2 + j // 2
+            if late < TOK_TILES:
+                if j % 2 == 0:
+                    late_rows = normalise(late)
+                else:
+                    pack_tokens(late, late_rows)
+
+        for j in range(GROUPS):
+            for i in range(2, TOK_TILES):
+                multiply(i, j, nc.sync)

@@ -50,7 +50,6 @@ def tile_attentionlayerdecoder_pa_kernel(
         grouped_pool = ctx.enter_context(tc.tile_pool(name="grouped", bufs=PASSES))
         result_pool = ctx.enter_context(tc.tile_pool(name="result", bufs=8))
         psum = ctx.enter_context(tc.psum_pool(name="psum", bufs=8))
-        ctx.enter_context(tc.manual_schedule())
 
         gain_row = keep.tile([P, HD], BF16)
         nc.vector.memset(gain_row[:].bitcast(I32), 0)

@@ -50,6 +50,7 @@ def tile_attentionlayerdecoder_pa_kernel(
         grouped_pool = ctx.enter_context(tc.tile_pool(name="grouped", bufs=PASSES))
         result_pool = ctx.enter_context(tc.tile_pool(name="result", bufs=8))
         psum = ctx.enter_context(tc.psum_pool(name="psum", bufs=8))
+        ctx.enter_context(tc.manual_schedule())
 
         gain_row = keep.tile([P, HD], BF16)
         nc.vector.memset(gain_row[:].bitcast(I32), 0)
@@ -215,10 +216,10 @@ def tile_attentionlayerdecoder_pa_kernel(
         load_tokens(1)
         load_biases()
         load_weights(0)
+        load_weights(1)
         load_tokens(2)
+        load_weights(2)
         load_tokens(3)
-        for j in range(1, RAW_GROUPS):
-            load_weights(j)
 
         broadcast_gain()
         x_rows_0 = normalise(0)
@@ -230,23 +231,31 @@ def tile_attentionlayerdecoder_pa_kernel(
         prepare_weights(0, 1)
         load_weights(RAW_GROUPS)
 
+        def lag(i):
+            return 2 * max(0, i - 1)
+
         late_rows = None
-        for j in range(GROUPS):
-            if j + 1 < GROUPS:
-                broadcast_bias(j + 1)
-            for half in range(2):
-                if j + 1 < GROUPS:
-                    prepare_weights(j + 1, half)
-                multiply(half, j, nc.gpsimd)
-            if j + 1 + RAW_GROUPS < GROUPS:
-                load_weights(j + 1 + RAW_GROUPS)
-            late = 2 + j // 2
+        for step in range(GROUPS + lag(TOK_TILES - 1)):
+            products = [
+                (i, step - lag(i)) for i in range(TOK_TILES) if 0 <= step - lag(i) < GROUPS
+            ]
+            first_half = (len(products) + 1) // 2
+            preparing = step + 1 < GROUPS
+            store_queue = nc.gpsimd if preparing else nc.sync
+            if preparing:
+                broadcast_bias(step + 1)
+                prepare_weights(step + 1, 0)
+            for i, j in products[:first_half]:
+                multiply(i, j, store_queue)
+            if preparing:
+                prepare_weights(step + 1, 1)
+            for i, j in products[first_half:]:
+                multiply(i, j, store_queue)
+            if step + 1 + RAW_GROUPS < GROUPS:
+                load_weights(step + 1 + RAW_GROUPS)
+            late = 2 + step // 2
             if late < TOK_TILES:
-                if j % 2 == 0:
+                if step % 2 == 0:
                     late_rows = normalise(late)
                 else:
                     pack_tokens(late, late_rows)
-
-        for j in range(GROUPS):
-            for i in range(2, TOK_TILES):
-                multiply(i, j, nc.sync)

@@ -173,7 +173,9 @@ def tile_attentionlayerdecoder_pa_kernel(
                             in_=raw_heads[(j, 2 * pair + r)][:].bitcast(F32)[:, first : first + P],
                             identity=ident_f32[:],
                         )
-                nc.scalar.copy(
+                last_bank = g == PASSES - 1 and pair == HEADS // 2 - 1
+                copy = nc.vector.tensor_copy if last_bank else nc.scalar.copy
+                copy(
                     out=words[:, 2 * pair * P : 2 * (pair + 1) * P, :],
                     in_=bank[:].rearrange("p u o -> p o u"),
                 )

from contextlib import ExitStack

import concourse.mybir as mybir
from concourse.masks import make_identity

F32 = mybir.dt.float32
BF16 = mybir.dt.bfloat16
I32 = mybir.dt.int32
U32 = mybir.dt.uint32
U8 = mybir.dt.uint8
FP8X4 = mybir.dt.float8_e4m3fn_x4
ACT = mybir.ActivationFunctionType
ALU = mybir.AluOpType

P = 128
PACK = 4
K_PASS = P * PACK
N_TOK = 512
HD = 2048
PASSES = HD // K_PASS
TOK_TILES = N_TOK // P
GROUP = 512
HEADS = GROUP // P
Q_GROUPS = 4
GROUPS = Q_GROUPS + 2
RAW_GROUPS = 3
EPS = 2.0 ** -23

FLOPS = 2 * N_TOK * GROUPS * GROUP * HD


def tile_attentionlayerdecoder_pa_kernel(
    tc, tokens, norm_w, Wq, bq, Wk, bk, Wv, bv, out_0, out_1, out_2
):
    nc = tc.nc
    token_rows = tokens.rearrange("b n k -> (b n) k")
    q_heads = out_0.rearrange("b h n d -> (b h) n d")

    group_rows = [Wq[q * GROUP : (q + 1) * GROUP, :] for q in range(Q_GROUPS)] + [Wk, Wv]
    group_heads = [q_heads[q * HEADS : (q + 1) * HEADS, :, :] for q in range(Q_GROUPS)] + [
        out_1.rearrange("b h n d -> (b h) n d"),
        out_2.rearrange("b h n d -> (b h) n d"),
    ]

    with ExitStack() as ctx:
        keep = ctx.enter_context(tc.tile_pool(name="keep", bufs=1))
        raw_pool = ctx.enter_context(tc.tile_pool(name="raw", bufs=RAW_GROUPS * HEADS))
        stats = ctx.enter_context(tc.tile_pool(name="stats", bufs=TOK_TILES))
        rows_pool = ctx.enter_context(tc.tile_pool(name="rows", bufs=2))
        grouped_pool = ctx.enter_context(tc.tile_pool(name="grouped", bufs=PASSES))
        result_pool = ctx.enter_context(tc.tile_pool(name="result", bufs=8))
        psum = ctx.enter_context(tc.psum_pool(name="psum", bufs=8))
        ctx.enter_context(tc.manual_schedule())

        gain_row = keep.tile([P, HD], BF16)
        nc.vector.memset(gain_row[:].bitcast(I32), 0)
        ones = keep.tile([P, P], BF16)
        nc.vector.memset(ones[:], 1.0)
        eps_col = keep.tile([P, 1], F32)
        nc.vector.memset(eps_col[:], EPS)
        bias_row = keep.tile([P, GROUPS * GROUP], BF16)
        nc.vector.memset(bias_row[:].bitcast(I32), 0)
        ident_bf16 = keep.tile([P, P], BF16)
        make_identity(nc, ident_bf16[:])
        ident_f32 = keep.tile([P, P], F32)
        make_identity(nc, ident_f32[:])

        warm = keep.tile([P, 1], F32)
        nc.scalar.activation(out=warm[:], in_=eps_col[:], func=ACT.Sqrt)

        def load_gain():
            nc.sync.dma_start(out=gain_row[0:1, :], in_=norm_w.rearrange("(o k) -> o k", o=1))

        def load_biases():
            first = 0
            for bias in (bq, bk, bv):
                width = bias.shape[0]
                nc.sync.dma_start(
                    out=bias_row[0:1, first : first + width],
                    in_=bias.rearrange("(o c) -> o c", o=1),
                )
                first += width

        gain_all = keep.tile([P, HD], BF16)
        bias_all = keep.tile([P, GROUPS * GROUP], F32)
        x_codes = keep.tile([P, TOK_TILES, PASSES, P], U32, align_bytes=64)
        x_scales = keep.tile([P, TOK_TILES, PASSES, P], U8, align_bytes=64)
        w_codes = [
            keep.tile([P, PASSES, GROUP], U32, name="w_codes%d" % j, align_bytes=64)
            for j in range(GROUPS)
        ]
        w_scales = [
            keep.tile([P, PASSES, GROUP], U8, name="w_scales%d" % j, align_bytes=64)
            for j in range(GROUPS)
        ]
        token_tiles = [keep.tile([P, HD], BF16, name="tokens%d" % i) for i in range(TOK_TILES)]
        raw_heads = {}

        def load_tokens(i):
            nc.sync.dma_start(out=token_tiles[i][:], in_=token_rows[i * P : (i + 1) * P, :])

        def load_weights(j):
            for h in range(HEADS):
                head = raw_pool.tile([P, HD], BF16, name="raw_head", tag="raw_head")
                nc.sync.dma_start(out=head[:], in_=group_rows[j][h * P : (h + 1) * P, :])
                raw_heads[(j, h)] = head

        def broadcast_gain():
            for c in range(HD // GROUP):
                cols = slice(c * GROUP, (c + 1) * GROUP)
                bank = psum.tile([P, GROUP], F32, tag="bank")
                nc.tensor.matmul(out=bank[:], lhsT=ones[:], rhs=gain_row[:, cols], start=True, stop=True)
                nc.vector.tensor_copy(out=gain_all[:, cols], in_=bank[:])

        def broadcast_bias(j):
            cols = slice(j * GROUP, (j + 1) * GROUP)
            bank = psum.tile([P, GROUP], F32, tag="bank")
            nc.tensor.matmul(out=bank[:], lhsT=ones[:], rhs=bias_row[:, cols], start=True, stop=True)
            nc.scalar.copy(out=bias_all[:, cols], in_=bank[:])

        def normalise(i):
            squares = rows_pool.tile([P, HD], BF16, tag="squares")
            sum_sq = stats.tile([P, 1], F32, tag="sum_sq")
            nc.scalar.activation(
                out=squares[:], in_=token_tiles[i][:], func=ACT.Square, accum_out=sum_sq[:]
            )
            rms = stats.tile([P, 1], F32, tag="rms")
            nc.scalar.activation(
                out=rms[:], in_=sum_sq[:], func=ACT.Sqrt, scale=1.0 / HD, bias=eps_col[:]
            )
            rstd = stats.tile([P, 1], F32, tag="rstd")
            nc.vector.reciprocal(out=rstd[:], in_=rms[:])
            x_rows = rows_pool.tile([P, HD], BF16, tag="x_rows")
            by_parity = "n (c p e) -> n c p e"
            for e in range(2):
                nc.vector.scalar_tensor_tensor(
                    out=x_rows[:].rearrange("n (c e p) -> n c e p", e=2, p=P)[:, :, e, :],
                    in0=token_tiles[i][:].rearrange(by_parity, p=P, e=2)[:, :, :, e],
                    scalar=rstd[:, 0:1],
                    in1=gain_all[:].rearrange(by_parity, p=P, e=2)[:, :, :, e],
                    op0=ALU.mult,
                    op1=ALU.mult,
                )
            return x_rows

        def pack_tokens(i, x_rows):
            grouped = rows_pool.tile([P, PASSES, P, PACK], BF16, tag="grouped_x", align_bytes=64)
            for g in range(PASSES):
                bank = psum.tile([P, PACK, P], BF16, tag="bank")
                for t in range(PACK):
                    first = (g * PACK + t) * P
                    nc.tensor.transpose(
                        out=bank[:, t, :], in_=x_rows[:, first : first + P], identity=ident_bf16[:]
                    )
                copy = nc.scalar.copy if g % 2 == 0 else nc.vector.tensor_copy
                copy(out=grouped[:, g, :, :], in_=bank[:].rearrange("p t n -> p n t"))
            nc.vector.quantize_mx(
                out=x_codes[:, i, :, :].rearrange("p g n -> p (g n)").bitcast(FP8X4),
                scales=x_scales[:, i, :, :].rearrange("p g n -> p (g n)"),
                in_=grouped[:].rearrange("p g n t -> p (g n t)"),
            )

        def transpose_weights(j, g):
            grouped = grouped_pool.tile([P, GROUP * PACK], BF16, tag="grouped_w", align_bytes=64)
            words = grouped[:].bitcast(F32).rearrange("p (o u) -> p o u", u=2)
            for pair in range(HEADS // 2):
                bank = psum.tile([P, 2, 2 * P], F32, tag="bank")
                for u in range(2):
                    first = (2 * g + u) * P
                    for r in range(2):
                        nc.tensor.transpose(
                            out=bank[:, u, r * P : (r + 1) * P],
                            in_=raw_heads[(j, 2 * pair + r)][:].bitcast(F32)[:, first : first + P],
                            identity=ident_f32[:],
                        )
                last_bank = g == PASSES - 1 and pair == HEADS // 2 - 1
                copy = nc.vector.tensor_copy if last_bank else nc.scalar.copy
                copy(
                    out=words[:, 2 * pair * P : 2 * (pair + 1) * P, :],
                    in_=bank[:].rearrange("p u o -> p o u"),
                )
            return grouped

        def quantise_weights(j, g, grouped):
            nc.vector.quantize_mx(
                out=w_codes[j][:, g, :].bitcast(FP8X4), scales=w_scales[j][:, g, :], in_=grouped[:]
            )

        def multiply(i, j, store_queue):
            bank = psum.tile([P, GROUP], F32, tag="bank")
            for g in range(PASSES):
                nc.tensor.matmul_mx(
                    out=bank[:],
                    lhsT=x_codes[:, i, g, :].bitcast(FP8X4),
                    lhsT_scale=x_scales[:, i, g, :],
                    rhs=w_codes[j][:, g, :].bitcast(FP8X4),
                    rhs_scale=w_scales[j][:, g, :],
                    start=(g == 0),
                    stop=(g == PASSES - 1),
                )
            result = result_pool.tile([P, GROUP], F32, tag="result")
            nc.vector.tensor_tensor(
                out=result[:], in0=bank[:], in1=bias_all[:, j * GROUP : (j + 1) * GROUP], op=ALU.add
            )
            store_queue.dma_start(
                out=group_heads[j][:, i * P : (i + 1) * P, :].rearrange("h n d -> n h d"),
                in_=result[:].rearrange("n (h d) -> n h d", h=HEADS),
            )

        def prepare_weights(j, half):
            passes = (2 * half, 2 * half + 1)
            grouped = [transpose_weights(j, g) for g in passes]
            for g, tile_g in zip(passes, grouped):
                quantise_weights(j, g, tile_g)

        load_gain()
        load_tokens(0)
        load_tokens(1)
        load_biases()
        load_weights(0)
        load_weights(1)
        load_tokens(2)
        load_weights(2)
        load_tokens(3)

        broadcast_gain()
        x_rows_0 = normalise(0)
        x_rows_1 = normalise(1)
        pack_tokens(0, x_rows_0)
        broadcast_bias(0)
        prepare_weights(0, 0)
        pack_tokens(1, x_rows_1)
        prepare_weights(0, 1)
        load_weights(RAW_GROUPS)

        def lag(i):
            return 2 * max(0, i - 1)

        late_rows = None
        for step in range(GROUPS + lag(TOK_TILES - 1)):
            products = [
                (i, step - lag(i)) for i in range(TOK_TILES) if 0 <= step - lag(i) < GROUPS
            ]
            first_half = (len(products) + 1) // 2
            preparing = step + 1 < GROUPS
            store_queue = nc.gpsimd if preparing else nc.sync
            if preparing:
                broadcast_bias(step + 1)
                prepare_weights(step + 1, 0)
            for i, j in products[:first_half]:
                multiply(i, j, store_queue)
            if preparing:
                prepare_weights(step + 1, 1)
            for i, j in products[first_half:]:
                multiply(i, j, store_queue)
            if step + 1 + RAW_GROUPS < GROUPS:
                load_weights(step + 1 + RAW_GROUPS)
            late = 2 + step // 2
            if late < TOK_TILES:
                if step % 2 == 0:
                    late_rows = normalise(late)
                else:
                    pack_tokens(late, late_rows)
